import numpy as np
import ml_dtypes


def mxq(x, axis, fmt="e4m3"):
    dtype, down = {"e4m3": (ml_dtypes.float8_e4m3fn, 7), "e5m2": (ml_dtypes.float8_e5m2, 14)}[fmt]
    v = np.moveaxis(np.asarray(x, np.float32).astype(ml_dtypes.bfloat16).astype(np.float64), axis, -1)
    blocks = v.reshape(v.shape[:-1] + (-1, 32))
    amax = np.abs(blocks).max(-1, keepdims=True)
    byte = np.maximum(np.where(amax > 0, np.frexp(amax)[1] - 1 + 127, 0) - down, 1)
    scale = np.exp2(byte - 127.0)
    codes = (blocks / scale).astype(np.float32).astype(dtype).astype(np.float64)
    return np.moveaxis((codes * scale).reshape(v.shape), -1, axis)


WIDE = False


def mx_kscale(k):
    if not WIDE:
        return np.ones(k)
    levels = np.array([10, -10, 5, -5, 0])
    a = np.random.permutation(np.resize(levels, k // 512 * 4)).reshape(k // 512, 4)
    idx = np.arange(k)
    return np.exp2(a[idx // 512, idx % 128 // 32])


BF16 = ml_dtypes.bfloat16


def bf(x):
    return np.asarray(x, np.float32).astype(BF16)


def f64(x):
    return np.asarray(x).astype(np.float64)


B, S, D, P, N1, N2, N3 = 4, 1024, 1024, 128, 2, 1, 1
H = N1 + N2 + N3


def setup_inputs():
    s = mx_kscale(D)
    a = 1.0 / np.sqrt(D)
    return {"x": bf(np.random.standard_normal((B, S, D)) * s),
            "w_now": bf(np.random.standard_normal((H, P, D)) * a / s),
            "w_back1": bf(np.random.standard_normal((N2 + N3, P, D)) * a / s),
            "w_back2": bf(np.random.standard_normal((N3, P, D)) * a / s),
            "bias": bf(np.random.standard_normal((H, P)) * 0.5)}


def reference(x, w_now, w_back1, w_back2, bias):
    xq = mxq(f64(x), 2, "e4m3")
    y = 0.0
    for j, w in enumerate((w_now, w_back1, w_back2)):
        z = xq @ mxq(f64(w), 2, "e4m3").reshape(-1, D).T
        y = y + np.pad(z[:, :S - j], ((0, 0), (j, 0), (H * P - z.shape[-1], 0)))
    return y.reshape(B, S, H, P).transpose(0, 2, 1, 3) + f64(bias)[None, :, None, :]

@@ -1,0 +1,173 @@
+from contextlib import ExitStack
+
+import concourse.mybir as mybir
+from concourse.masks import make_identity
+
+F32 = mybir.dt.float32
+BF16 = mybir.dt.bfloat16
+U32 = mybir.dt.uint32
+U8 = mybir.dt.uint8
+FP8X4 = mybir.dt.float8_e4m3fn_x4
+
+P = 128
+SEQS = 4
+S = 1024
+D = 1024
+HEADS = 4
+BLOCKS = S // P
+PASSES = D // (4 * P)
+WORDS = D // 2
+CHUNKS = WORDS // P
+LOOKBACK = 2
+SLOTS = BLOCKS + LOOKBACK
+RUN = 4
+ROUNDS = SEQS * BLOCKS // RUN
+
+TAP_COLS = (4 * P, 2 * P, 1 * P)
+TAP_START = (0, 4 * P, 6 * P)
+W_COLS = 7 * P
+
+FLOPS = 2 * SEQS * S * D * W_COLS
+
+
+def tile_multiheadhomogeneousattention_pa_t_kernel(tc, x, w_now, w_back1, w_back2, bias, out):
+    nc = tc.nc
+    with ExitStack() as ctx:
+        ctx.enter_context(tc.manual_schedule())
+        keep = ctx.enter_context(tc.tile_pool(name="keep", bufs=1))
+        stage = ctx.enter_context(tc.tile_pool(name="stage", bufs=4))
+        quant = ctx.enter_context(tc.tile_pool(name="quant", bufs=2))
+        results = ctx.enter_context(tc.tile_pool(name="results", bufs=3))
+        flipped = ctx.enter_context(tc.psum_pool(name="flipped", bufs=4))
+        sums = ctx.enter_context(tc.psum_pool(name="sums", bufs=4))
+
+        w_rows = [w_now[0], w_now[1], w_now[2], w_now[3], w_back1[0], w_back1[1], w_back2[0]]
+        w_sb = keep.tile([P, len(w_rows) * D], BF16)
+        for b, rows in enumerate(w_rows):
+            nc.sync.dma_start(out=w_sb[:, b * D : (b + 1) * D], in_=rows)
+        x_sb = []
+        for n in range(SEQS):
+            x_seq = keep.tile([P, BLOCKS * D], BF16, name="x_sb%d" % n)
+            x_sb.append(x_seq)
+            tokens = x[n].rearrange("(i j) k -> i (j k)", j=BLOCKS)
+            for pair in range(BLOCKS // 2):
+                j = transposed_block(2 * pair)
+                nc.sync.dma_start(out=x_seq[:, j * D : (j + 2) * D], in_=tokens[:, j * D : (j + 2) * D])
+
+        ident = keep.tile([P, P], F32)
+        make_identity(nc, ident[:])
+        ones = keep.tile([P, P], BF16)
+        nc.vector.memset(ones[:], 1.0)
+        bias_rows = keep.tile([P, HEADS * P], BF16)
+        nc.vector.memset(bias_rows[:], 0.0)
+        nc.scalar.dma_start(out=bias_rows[0:1, :], in_=bias.rearrange("h c -> (h c)").unsqueeze(0))
+        shifted = {}
+        for j in range(BLOCKS - LOOKBACK, BLOCKS):
+            shifted[j] = keep.tile([P, PASSES * P * 4], BF16, name="shifted%d" % j, align_bytes=64)
+            nc.vector.memset(shifted[j][:], 0.0)
+
+        def flip(rows_f32):
+            bank = flipped.tile([P, CHUNKS, P], F32, name="bank")
+            for c in range(CHUNKS):
+                nc.tensor.transpose(bank[:, c, :], rows_f32[:, c * P : (c + 1) * P], ident[:])
+            return bank[:].rearrange("p (g u) r -> p g r u", u=2)
+
+        w_f32 = w_sb[:].bitcast(F32)
+        w_grouped = keep.tile([P, PASSES * W_COLS * 4], BF16, align_bytes=64)
+        w_grouped_f32 = w_grouped[:].bitcast(F32).rearrange("p (g r u) -> p g r u", g=PASSES, u=2)
+        w_codes = keep.tile([P, PASSES * W_COLS], U32, align_bytes=64)
+        w_scales = keep.tile([P, PASSES * W_COLS], U8, align_bytes=64)
+        for start, cols in zip(TAP_START, TAP_COLS):
+            for b in range(start // P, (start + cols) // P):
+                words = flip(w_f32[:, b * WORDS : (b + 1) * WORDS])
+                if b % 2 == 0:
+                    nc.scalar.copy(out=w_grouped_f32[:, :, b * P : (b + 1) * P, :], in_=words)
+                else:
+                    nc.vector.tensor_copy(out=w_grouped_f32[:, :, b * P : (b + 1) * P, :], in_=words)
+            for g in range(PASSES):
+                first = g * W_COLS + start
+                nc.vector.quantize_mx(
+                    out=w_codes[:, first : first + cols].bitcast(FP8X4),
+                    scales=w_scales[:, first : first + cols],
+                    in_=w_grouped[:, 4 * first : 4 * (first + cols)],
+                )
+
+        bias_sum = sums.tile([P, HEADS * P], F32, name="acc")
+        nc.tensor.matmul(out=bias_sum[:], lhsT=ones[:], rhs=bias_rows[:], start=True, stop=True)
+        bias_all = keep.tile([P, HEADS * P], F32)
+        nc.vector.tensor_copy(out=bias_all[:], in_=bias_sum[:])
+
+        codes = {}
+        scales = {}
+        grouped = {}
+
+        def transpose_block(position):
+            n, j = position // BLOCKS, transposed_block(position % BLOCKS)
+            words = flip(x_sb[n][:].bitcast(F32)[:, j * WORDS : (j + 1) * WORDS])
+            plain = stage.tile([P, PASSES * P * 4], BF16, name="plain", align_bytes=64)
+            grouped[position] = plain
+            nc.scalar.copy(out=plain[:].bitcast(F32).rearrange("p (g i u) -> p g i u", g=PASSES, u=2), in_=words)
+            if j in shifted:
+                moved = shifted[j][:].bitcast(F32).rearrange("p (g i u) -> p g i u", g=PASSES, u=2)
+                nc.scalar.copy(out=moved[:, :, 1:P, :], in_=words[:, :, 0 : P - 1, :])
+
+        def quantise(n, slot, values):
+            width = PASSES * P
+            nc.vector.quantize_mx(
+                out=codes[n][:, slot * width : (slot + 1) * width].bitcast(FP8X4),
+                scales=scales[n][:, slot * width : (slot + 1) * width],
+                in_=values[:],
+            )
+
+        def quantise_block(position):
+            n, j = position // BLOCKS, transposed_block(position % BLOCKS)
+            if position % BLOCKS == 0:
+                codes[n] = quant.tile([P, SLOTS * PASSES * P], U32, name="codes", align_bytes=64)
+                scales[n] = quant.tile([P, SLOTS * PASSES * P], U8, name="scales", align_bytes=64)
+            quantise(n, j, grouped[position])
+            if j in shifted:
+                quantise(n, j + LOOKBACK, shifted[j])
+
+        def project_block(n, j, result):
+            acc = sums.tile([P, HEADS * P], F32, name="acc")
+            for tap, (start, cols) in enumerate(zip(TAP_START, TAP_COLS)):
+                slot = j - tap if j >= tap else j - tap + BLOCKS + LOOKBACK
+                for g in range(PASSES):
+                    tokens = (slot * PASSES + g) * P
+                    first = g * W_COLS + start
+                    nc.tensor.matmul_mx(
+                        out=acc[:, HEADS * P - cols :],
+                        lhsT=codes[n][:, tokens : tokens + P].bitcast(FP8X4),
+                        lhsT_scale=scales[n][:, tokens : tokens + P],
+                        rhs=w_codes[:, first : first + cols].bitcast(FP8X4),
+                        rhs_scale=w_scales[:, first : first + cols],
+                        start=(tap == 0 and g == 0),
+                        stop=(tap == LOOKBACK and g == PASSES - 1),
+                    )
+            nc.vector.tensor_tensor(
+                out=result[:, :, j % RUN, :],
+                in0=acc[:].rearrange("p (h c) -> p h c", h=HEADS),
+                in1=bias_all[:].rearrange("p (h c) -> p h c", h=HEADS),
+                op=mybir.AluOpType.add,
+            )
+
+        for r in range(ROUNDS + 1):
+            if r < ROUNDS:
+                for b in range(RUN):
+                    transpose_block(r * RUN + b)
+            if r > 0:
+                result = results.tile([P, HEADS, RUN, P], F32, name="result")
+            for b in range(RUN):
+                if r < ROUNDS:
+                    quantise_block(r * RUN + b)
+                if r > 0:
+                    m = (r - 1) * RUN + b
+                    project_block(m // BLOCKS, m % BLOCKS, result)
+            if r > 0:
+                m = (r - 1) * RUN
+                rows = out[m // BLOCKS].rearrange("h (i j) c -> i h j c", j=BLOCKS)
+                nc.sync.dma_start(out=rows[:, :, m % BLOCKS : m % BLOCKS + RUN, :], in_=result[:])
+
+
+def transposed_block(position):
+    return (position - LOOKBACK) % BLOCKS

@@ -157,16 +157,19 @@ def tile_multiheadhomogeneousattention_pa_t_kernel(tc, x, w_now, w_back1, w_back
                     transpose_block(r * RUN + b)
             if r > 0:
                 result = results.tile([P, HEADS, RUN, P], F32, name="result")
+            stored = 1 if r == ROUNDS else RUN
             for b in range(RUN):
                 if r < ROUNDS:
                     quantise_block(r * RUN + b)
                 if r > 0:
                     m = (r - 1) * RUN + b
-                    project_block(m // BLOCKS, m % BLOCKS, result)
-            if r > 0:
-                m = (r - 1) * RUN
-                rows = out[m // BLOCKS].rearrange("h (i j) c -> i h j c", j=BLOCKS)
-                nc.sync.dma_start(out=rows[:, :, m % BLOCKS : m % BLOCKS + RUN, :], in_=result[:])
+                    n, j = m // BLOCKS, m % BLOCKS
+                    project_block(n, j, result)
+                    if (b + 1) % stored == 0:
+                        rows = out[n].rearrange("h (i j) c -> i h j c", j=BLOCKS)
+                        nc.sync.dma_start(
+                            out=rows[:, :, j + 1 - stored : j + 1, :], in_=result[:, :, b + 1 - stored : b + 1, :]
+                        )
 
 
 def transposed_block(position):

@@ -21,7 +21,10 @@ CHUNKS = WORDS // P
 LOOKBACK = 2
 SLOTS = BLOCKS + LOOKBACK
 RUN = 4
-ROUNDS = SEQS * BLOCKS // RUN
+ALL_BLOCKS = SEQS * BLOCKS
+T_RUN = 6
+T_BANKS = 5
+LAG = 5
 
 TAP_COLS = (4 * P, 2 * P, 1 * P)
 TAP_START = (0, 4 * P, 6 * P)
@@ -35,11 +38,11 @@ def tile_multiheadhomogeneousattention_pa_t_kernel(tc, x, w_now, w_back1, w_back
     with ExitStack() as ctx:
         ctx.enter_context(tc.manual_schedule())
         keep = ctx.enter_context(tc.tile_pool(name="keep", bufs=1))
-        stage = ctx.enter_context(tc.tile_pool(name="stage", bufs=4))
+        stage = ctx.enter_context(tc.tile_pool(name="stage", bufs=T_RUN + 2))
         quant = ctx.enter_context(tc.tile_pool(name="quant", bufs=2))
         results = ctx.enter_context(tc.tile_pool(name="results", bufs=3))
-        flipped = ctx.enter_context(tc.psum_pool(name="flipped", bufs=4))
-        sums = ctx.enter_context(tc.psum_pool(name="sums", bufs=4))
+        flipped = ctx.enter_context(tc.psum_pool(name="flipped", bufs=T_BANKS))
+        sums = ctx.enter_context(tc.psum_pool(name="sums", bufs=8 - T_BANKS))
 
         w_rows = [w_now[0], w_now[1], w_now[2], w_now[3], w_back1[0], w_back1[1], w_back2[0]]
         w_sb = keep.tile([P, len(w_rows) * D], BF16)
@@ -151,25 +154,34 @@ def tile_multiheadhomogeneousattention_pa_t_kernel(tc, x, w_now, w_back1, w_back
                 op=mybir.AluOpType.add,
             )
 
-        for r in range(ROUNDS + 1):
-            if r < ROUNDS:
-                for b in range(RUN):
-                    transpose_block(r * RUN + b)
-            if r > 0:
-                result = results.tile([P, HEADS, RUN, P], F32, name="result")
-            stored = 1 if r == ROUNDS else RUN
-            for b in range(RUN):
-                if r < ROUNDS:
-                    quantise_block(r * RUN + b)
-                if r > 0:
-                    m = (r - 1) * RUN + b
-                    n, j = m // BLOCKS, m % BLOCKS
-                    project_block(n, j, result)
-                    if (b + 1) % stored == 0:
-                        rows = out[n].rearrange("h (i j) c -> i h j c", j=BLOCKS)
-                        nc.sync.dma_start(
-                            out=rows[:, :, j + 1 - stored : j + 1, :], in_=result[:, :, b + 1 - stored : b + 1, :]
-                        )
+        result_of = {}
+        projected = 0
+        for first in range(0, ALL_BLOCKS, T_RUN):
+            transposed = min(first + T_RUN, ALL_BLOCKS)
+            for position in range(first, transposed):
+                transpose_block(position)
+            until = ALL_BLOCKS if transposed == ALL_BLOCKS else transposed - LAG
+            quantise_block(first)
+            quantised = first + 1
+            for m in range(projected, until):
+                wanted = min(transposed, max(quantised + 1, m + LOOKBACK + 1))
+                for position in range(quantised, wanted):
+                    quantise_block(position)
+                quantised = max(quantised, wanted)
+                n, j, b = m // BLOCKS, m % BLOCKS, m % RUN
+                if b == 0:
+                    result_of[m // RUN] = results.tile([P, HEADS, RUN, P], F32, name="result")
+                result = result_of[m // RUN]
+                project_block(n, j, result)
+                stored = 1 if m >= ALL_BLOCKS - RUN else RUN
+                if (b + 1) % stored == 0:
+                    rows = out[n].rearrange("h (i j) c -> i h j c", j=BLOCKS)
+                    nc.sync.dma_start(
+                        out=rows[:, :, j + 1 - stored : j + 1, :], in_=result[:, :, b + 1 - stored : b + 1, :]
+                    )
+            projected = max(projected, until)
+            for position in range(quantised, transposed):
+                quantise_block(position)
 
 
 def transposed_block(position):

@@ -22,9 +22,9 @@ LOOKBACK = 2
 SLOTS = BLOCKS + LOOKBACK
 RUN = 4
 ALL_BLOCKS = SEQS * BLOCKS
-T_RUN = 6
-T_BANKS = 5
-LAG = 5
+T_RUN = 3
+T_BANKS = 4
+LAG = 4
 
 TAP_COLS = (4 * P, 2 * P, 1 * P)
 TAP_START = (0, 4 * P, 6 * P)

@@ -53,9 +53,12 @@ def tile_multiheadhomogeneousattention_pa_t_kernel(tc, x, w_now, w_back1, w_back
             x_seq = keep.tile([P, BLOCKS * D], BF16, name="x_sb%d" % n)
             x_sb.append(x_seq)
             tokens = x[n].rearrange("(i j) k -> i (j k)", j=BLOCKS)
-            for pair in range(BLOCKS // 2):
-                j = transposed_block(2 * pair)
-                nc.sync.dma_start(out=x_seq[:, j * D : (j + 2) * D], in_=tokens[:, j * D : (j + 2) * D])
+            together = 1 if n == 0 else 2
+            for position in range(0, BLOCKS, together):
+                j = transposed_block(position)
+                nc.sync.dma_start(
+                    out=x_seq[:, j * D : (j + together) * D], in_=tokens[:, j * D : (j + together) * D]
+                )
 
         ident = keep.tile([P, P], F32)
         make_identity(nc, ident[:])
@@ -78,8 +81,10 @@ def tile_multiheadhomogeneousattention_pa_t_kernel(tc, x, w_now, w_back1, w_back
         w_f32 = w_sb[:].bitcast(F32)
         w_grouped = keep.tile([P, PASSES * W_COLS * 4], BF16, align_bytes=64)
         w_grouped_f32 = w_grouped[:].bitcast(F32).rearrange("p (g r u) -> p g r u", g=PASSES, u=2)
-        w_codes = keep.tile([P, PASSES * W_COLS], U32, align_bytes=64)
-        w_scales = keep.tile([P, PASSES * W_COLS], U8, align_bytes=64)
+        w_codes_room = keep.tile([P, 128 // 4 + PASSES * W_COLS], U32, align_bytes=256)
+        w_codes = w_codes_room[:, 128 // 4 :]
+        w_scales_room = keep.tile([P, 192 + PASSES * W_COLS], U8, align_bytes=256)
+        w_scales = w_scales_room[:, 192:]
         for start, cols in zip(TAP_START, TAP_COLS):
             for b in range(start // P, (start + cols) // P):
                 words = flip(w_f32[:, b * WORDS : (b + 1) * WORDS])
@@ -125,8 +130,9 @@ def tile_multiheadhomogeneousattention_pa_t_kernel(tc, x, w_now, w_back1, w_back
         def quantise_block(position):
             n, j = position // BLOCKS, transposed_block(position % BLOCKS)
             if position % BLOCKS == 0:
-                codes[n] = quant.tile([P, SLOTS * PASSES * P], U32, name="codes", align_bytes=64)
-                scales[n] = quant.tile([P, SLOTS * PASSES * P], U8, name="scales", align_bytes=64)
+                codes[n] = quant.tile([P, SLOTS * PASSES * P], U32, name="codes", align_bytes=256)
+                scales_room = quant.tile([P, 64 + SLOTS * PASSES * P], U8, name="scales", align_bytes=256)
+                scales[n] = scales_room[:, 64:]
             quantise(n, j, grouped[position])
             if j in shifted:
                 quantise(n, j + LOOKBACK, shifted[j])

@@ -22,6 +22,7 @@ LOOKBACK = 2
 SLOTS = BLOCKS + LOOKBACK
 RUN = 4
 ALL_BLOCKS = SEQS * BLOCKS
+LAST_STORED = 2
 T_RUN = 3
 T_BANKS = 4
 LAG = 4
@@ -179,7 +180,7 @@ def tile_multiheadhomogeneousattention_pa_t_kernel(tc, x, w_now, w_back1, w_back
                     result_of[m // RUN] = results.tile([P, HEADS, RUN, P], F32, name="result")
                 result = result_of[m // RUN]
                 project_block(n, j, result)
-                stored = 1 if m >= ALL_BLOCKS - RUN else RUN
+                stored = LAST_STORED if m >= ALL_BLOCKS - RUN else RUN
                 if (b + 1) % stored == 0:
                     rows = out[n].rearrange("h (i j) c -> i h j c", j=BLOCKS)
                     nc.sync.dma_start(

@@ -23,7 +23,7 @@ SLOTS = BLOCKS + LOOKBACK
 RUN = 4
 ALL_BLOCKS = SEQS * BLOCKS
 LAST_STORED = 2
-T_RUN = 3
+T_RUN = 2
 T_BANKS = 4
 LAG = 4
 

from contextlib import ExitStack

import concourse.mybir as mybir
from concourse.masks import make_identity

F32 = mybir.dt.float32
BF16 = mybir.dt.bfloat16
U32 = mybir.dt.uint32
U8 = mybir.dt.uint8
FP8X4 = mybir.dt.float8_e4m3fn_x4

P = 128
SEQS = 4
S = 1024
D = 1024
HEADS = 4
BLOCKS = S // P
PASSES = D // (4 * P)
WORDS = D // 2
CHUNKS = WORDS // P
LOOKBACK = 2
SLOTS = BLOCKS + LOOKBACK
RUN = 4
ALL_BLOCKS = SEQS * BLOCKS
LAST_STORED = 2
T_RUN = 2
T_BANKS = 4
LAG = 4

TAP_COLS = (4 * P, 2 * P, 1 * P)
TAP_START = (0, 4 * P, 6 * P)
W_COLS = 7 * P

FLOPS = 2 * SEQS * S * D * W_COLS


def tile_multiheadhomogeneousattention_pa_t_kernel(tc, x, w_now, w_back1, w_back2, bias, out):
    nc = tc.nc
    with ExitStack() as ctx:
        ctx.enter_context(tc.manual_schedule())
        keep = ctx.enter_context(tc.tile_pool(name="keep", bufs=1))
        stage = ctx.enter_context(tc.tile_pool(name="stage", bufs=T_RUN + 2))
        quant = ctx.enter_context(tc.tile_pool(name="quant", bufs=2))
        results = ctx.enter_context(tc.tile_pool(name="results", bufs=3))
        flipped = ctx.enter_context(tc.psum_pool(name="flipped", bufs=T_BANKS))
        sums = ctx.enter_context(tc.psum_pool(name="sums", bufs=8 - T_BANKS))

        w_rows = [w_now[0], w_now[1], w_now[2], w_now[3], w_back1[0], w_back1[1], w_back2[0]]
        w_sb = keep.tile([P, len(w_rows) * D], BF16)
        for b, rows in enumerate(w_rows):
            nc.sync.dma_start(out=w_sb[:, b * D : (b + 1) * D], in_=rows)
        x_sb = []
        for n in range(SEQS):
            x_seq = keep.tile([P, BLOCKS * D], BF16, name="x_sb%d" % n)
            x_sb.append(x_seq)
            tokens = x[n].rearrange("(i j) k -> i (j k)", j=BLOCKS)
            together = 1 if n == 0 else 2
            for position in range(0, BLOCKS, together):
                j = transposed_block(position)
                nc.sync.dma_start(
                    out=x_seq[:, j * D : (j + together) * D], in_=tokens[:, j * D : (j + together) * D]
                )

        ident = keep.tile([P, P], F32)
        make_identity(nc, ident[:])
        ones = keep.tile([P, P], BF16)
        nc.vector.memset(ones[:], 1.0)
        bias_rows = keep.tile([P, HEADS * P], BF16)
        nc.vector.memset(bias_rows[:], 0.0)
        nc.scalar.dma_start(out=bias_rows[0:1, :], in_=bias.rearrange("h c -> (h c)").unsqueeze(0))
        shifted = {}
        for j in range(BLOCKS - LOOKBACK, BLOCKS):
            shifted[j] = keep.tile([P, PASSES * P * 4], BF16, name="shifted%d" % j, align_bytes=64)
            nc.vector.memset(shifted[j][:], 0.0)

        def flip(rows_f32):
            bank = flipped.tile([P, CHUNKS, P], F32, name="bank")
            for c in range(CHUNKS):
                nc.tensor.transpose(bank[:, c, :], rows_f32[:, c * P : (c + 1) * P], ident[:])
            return bank[:].rearrange("p (g u) r -> p g r u", u=2)

        w_f32 = w_sb[:].bitcast(F32)
        w_grouped = keep.tile([P, PASSES * W_COLS * 4], BF16, align_bytes=64)
        w_grouped_f32 = w_grouped[:].bitcast(F32).rearrange("p (g r u) -> p g r u", g=PASSES, u=2)
        w_codes_room = keep.tile([P, 128 // 4 + PASSES * W_COLS], U32, align_bytes=256)
        w_codes = w_codes_room[:, 128 // 4 :]
        w_scales_room = keep.tile([P, 192 + PASSES * W_COLS], U8, align_bytes=256)
        w_scales = w_scales_room[:, 192:]
        for start, cols in zip(TAP_START, TAP_COLS):
            for b in range(start // P, (start + cols) // P):
                words = flip(w_f32[:, b * WORDS : (b + 1) * WORDS])
                if b % 2 == 0:
                    nc.scalar.copy(out=w_grouped_f32[:, :, b * P : (b + 1) * P, :], in_=words)
                else:
                    nc.vector.tensor_copy(out=w_grouped_f32[:, :, b * P : (b + 1) * P, :], in_=words)
            for g in range(PASSES):
                first = g * W_COLS + start
                nc.vector.quantize_mx(
                    out=w_codes[:, first : first + cols].bitcast(FP8X4),
                    scales=w_scales[:, first : first + cols],
                    in_=w_grouped[:, 4 * first : 4 * (first + cols)],
                )

        bias_sum = sums.tile([P, HEADS * P], F32, name="acc")
        nc.tensor.matmul(out=bias_sum[:], lhsT=ones[:], rhs=bias_rows[:], start=True, stop=True)
        bias_all = keep.tile([P, HEADS * P], F32)
        nc.vector.tensor_copy(out=bias_all[:], in_=bias_sum[:])

        codes = {}
        scales = {}
        grouped = {}

        def transpose_block(position):
            n, j = position // BLOCKS, transposed_block(position % BLOCKS)
            words = flip(x_sb[n][:].bitcast(F32)[:, j * WORDS : (j + 1) * WORDS])
            plain = stage.tile([P, PASSES * P * 4], BF16, name="plain", align_bytes=64)
            grouped[position] = plain
            nc.scalar.copy(out=plain[:].bitcast(F32).rearrange("p (g i u) -> p g i u", g=PASSES, u=2), in_=words)
            if j in shifted:
                moved = shifted[j][:].bitcast(F32).rearrange("p (g i u) -> p g i u", g=PASSES, u=2)
                nc.scalar.copy(out=moved[:, :, 1:P, :], in_=words[:, :, 0 : P - 1, :])

        def quantise(n, slot, values):
            width = PASSES * P
            nc.vector.quantize_mx(
                out=codes[n][:, slot * width : (slot + 1) * width].bitcast(FP8X4),
                scales=scales[n][:, slot * width : (slot + 1) * width],
                in_=values[:],
            )

        def quantise_block(position):
            n, j = position // BLOCKS, transposed_block(position % BLOCKS)
            if position % BLOCKS == 0:
                codes[n] = quant.tile([P, SLOTS * PASSES * P], U32, name="codes", align_bytes=256)
                scales_room = quant.tile([P, 64 + SLOTS * PASSES * P], U8, name="scales", align_bytes=256)
                scales[n] = scales_room[:, 64:]
            quantise(n, j, grouped[position])
            if j in shifted:
                quantise(n, j + LOOKBACK, shifted[j])

        def project_block(n, j, result):
            acc = sums.tile([P, HEADS * P], F32, name="acc")
            for tap, (start, cols) in enumerate(zip(TAP_START, TAP_COLS)):
                slot = j - tap if j >= tap else j - tap + BLOCKS + LOOKBACK
                for g in range(PASSES):
                    tokens = (slot * PASSES + g) * P
                    first = g * W_COLS + start
                    nc.tensor.matmul_mx(
                        out=acc[:, HEADS * P - cols :],
                        lhsT=codes[n][:, tokens : tokens + P].bitcast(FP8X4),
                        lhsT_scale=scales[n][:, tokens : tokens + P],
                        rhs=w_codes[:, first : first + cols].bitcast(FP8X4),
                        rhs_scale=w_scales[:, first : first + cols],
                        start=(tap == 0 and g == 0),
                        stop=(tap == LOOKBACK and g == PASSES - 1),
                    )
            nc.vector.tensor_tensor(
                out=result[:, :, j % RUN, :],
                in0=acc[:].rearrange("p (h c) -> p h c", h=HEADS),
                in1=bias_all[:].rearrange("p (h c) -> p h c", h=HEADS),
                op=mybir.AluOpType.add,
            )

        result_of = {}
        projected = 0
        for first in range(0, ALL_BLOCKS, T_RUN):
            transposed = min(first + T_RUN, ALL_BLOCKS)
            for position in range(first, transposed):
                transpose_block(position)
            until = ALL_BLOCKS if transposed == ALL_BLOCKS else transposed - LAG
            quantise_block(first)
            quantised = first + 1
            for m in range(projected, until):
                wanted = min(transposed, max(quantised + 1, m + LOOKBACK + 1))
                for position in range(quantised, wanted):
                    quantise_block(position)
                quantised = max(quantised, wanted)
                n, j, b = m // BLOCKS, m % BLOCKS, m % RUN
                if b == 0:
                    result_of[m // RUN] = results.tile([P, HEADS, RUN, P], F32, name="result")
                result = result_of[m // RUN]
                project_block(n, j, result)
                stored = LAST_STORED if m >= ALL_BLOCKS - RUN else RUN
                if (b + 1) % stored == 0:
                    rows = out[n].rearrange("h (i j) c -> i h j c", j=BLOCKS)
                    nc.sync.dma_start(
                        out=rows[:, :, j + 1 - stored : j + 1, :], in_=result[:, :, b + 1 - stored : b + 1, :]
                    )
            projected = max(projected, until)
            for position in range(quantised, transposed):
                quantise_block(position)


def transposed_block(position):
    return (position - LOOKBACK) % BLOCKS
